import numpy as np
import ml_dtypes


def mxq(x, axis, fmt="e4m3"):
    dtype, down = {"e4m3": (ml_dtypes.float8_e4m3fn, 7), "e5m2": (ml_dtypes.float8_e5m2, 14)}[fmt]
    v = np.moveaxis(np.asarray(x, np.float32).astype(ml_dtypes.bfloat16).astype(np.float64), axis, -1)
    blocks = v.reshape(v.shape[:-1] + (-1, 32))
    amax = np.abs(blocks).max(-1, keepdims=True)
    byte = np.maximum(np.where(amax > 0, np.frexp(amax)[1] - 1 + 127, 0) - down, 1)
    scale = np.exp2(byte - 127.0)
    codes = (blocks / scale).astype(np.float32).astype(dtype).astype(np.float64)
    return np.moveaxis((codes * scale).reshape(v.shape), -1, axis)


WIDE = False


def mx_kscale(k):
    if not WIDE:
        return np.ones(k)
    levels = np.array([10, -10, 5, -5, 0])
    a = np.random.permutation(np.resize(levels, k // 512 * 4)).reshape(k // 512, 4)
    idx = np.arange(k)
    return np.exp2(a[idx // 512, idx % 128 // 32])


BF16 = ml_dtypes.bfloat16


def bf(x):
    return np.asarray(x, np.float32).astype(BF16)


def f64(x):
    return np.asarray(x).astype(np.float64)


E2M1 = np.array([0.0, 0.5, 1.0, 1.5, 2.0, 3.0, 4.0, 6.0, -0.0, -0.5, -1.0, -1.5, -2.0, -3.0, -4.0, -6.0])


def pack_weight(w, fmt):
    k, n = w.shape
    w = f64(bf(w)).reshape(k // 32, 32, n)
    amax = np.abs(w).max(1)
    if fmt == "e4m3":
        byte = np.frexp(amax)[1] - 1 + 127 - 7
    else:
        mant, ex = np.frexp(amax / 6.0)
        byte = np.where(mant > 0.5, ex, ex - 1) + 127
    byte = np.clip(np.where(amax > 0, byte, 1), 1, 254)
    scaled = (w * np.exp2(127.0 - byte)[:, None, :]).reshape(k, n).astype(np.float32)
    by_word = np.ascontiguousarray(scaled.reshape(k // 512, 128, 4, n).transpose(0, 1, 3, 2))
    if fmt == "e4m3":
        words = by_word.astype(ml_dtypes.float8_e4m3fn).view(np.uint8)
    else:
        c = by_word.astype(ml_dtypes.float4_e2m1fn).view(np.uint8) & 0xF
        words = c[..., 0::2] | (c[..., 1::2] << 4)
    return np.ascontiguousarray(words), np.ascontiguousarray(byte.astype(np.uint8).reshape(k // 512, 16, n))


def unpack_weight(words, scales, fmt):
    g, p, n, _ = words.shape
    if fmt == "e4m3":
        vals = np.ascontiguousarray(words).view(ml_dtypes.float8_e4m3fn).astype(np.float64)
    else:
        nib = np.empty((g, p, n, 4), np.uint8)
        nib[..., 0::2] = words & 0xF
        nib[..., 1::2] = words >> 4
        vals = E2M1[nib]
    vals = vals * np.repeat(np.exp2(scales.astype(np.float64) - 127.0), 8, axis=1)[..., None]
    return vals.transpose(0, 1, 3, 2).reshape(g * 512, n)


B, N_I, N_H1, N_H2, N_H3, N_H4 = 512, 1024, 1024, 1024, 2048, 1024
K1 = N_I + N_H1
FMT = "e4m3"


def sigmoid(v):
    return 1.0 / (1.0 + np.exp(-v))


def setup_inputs():
    s = mx_kscale(K1)

    def w(gain):
        wide = np.random.standard_normal((N_H1, K1)) * gain / np.sqrt(K1) / s[None, :]
        return pack_weight(wide.T, FMT)

    def b():
        return bf(np.random.standard_normal(N_H1) * 0.3)

    X = bf(np.random.standard_normal((B, N_I)) * s[:N_I])
    hidden1 = bf(np.random.standard_normal((B, N_H1)) * s[N_I:])
    cell1 = bf(np.random.standard_normal((B, N_H1)))
    Wf1_words, Wf1_scales = w(1.0)
    bf1 = b()
    Wi1_words, Wi1_scales = w(1.0)
    bi1 = b()
    Wc1_words, Wc1_scales = w(5.0 / 3.0)
    bc1 = b()
    Wo1_words, Wo1_scales = w(1.0)
    bo1 = b()
    return {"X": X,
            "hidden1": hidden1,
            "cell1": cell1,
            "Wf1_words": Wf1_words, "Wf1_scales": Wf1_scales, "bf1": bf1,
            "Wi1_words": Wi1_words, "Wi1_scales": Wi1_scales, "bi1": bi1,
            "Wc1_words": Wc1_words, "Wc1_scales": Wc1_scales, "bc1": bc1,
            "Wo1_words": Wo1_words, "Wo1_scales": Wo1_scales, "bo1": bo1}


def reference(X, hidden1, cell1, Wf1_words, Wf1_scales, bf1, Wi1_words, Wi1_scales, bi1,
              Wc1_words, Wc1_scales, bc1, Wo1_words, Wo1_scales, bo1):
    zq = mxq(np.concatenate([f64(X), f64(hidden1)], axis=1), 1, "e4m3")
    f = sigmoid((zq @ unpack_weight(Wf1_words, Wf1_scales, FMT)) + f64(bf1))
    i = sigmoid((zq @ unpack_weight(Wi1_words, Wi1_scales, FMT)) + f64(bi1))
    cand = np.tanh((zq @ unpack_weight(Wc1_words, Wc1_scales, FMT)) + f64(bc1))
    o = sigmoid((zq @ unpack_weight(Wo1_words, Wo1_scales, FMT)) + f64(bo1))
    h_new = o * np.tanh(cand)
    c_new = f * f64(cell1) + cand * i
    return h_new, c_new

@@ -1,0 +1,220 @@
+from contextlib import ExitStack
+
+import concourse.mybir as mybir
+from concourse.masks import make_identity
+
+F32 = mybir.dt.float32
+BF16 = mybir.dt.bfloat16
+I32 = mybir.dt.int32
+U32 = mybir.dt.uint32
+U8 = mybir.dt.uint8
+FP8X4 = mybir.dt.float8_e4m3fn_x4
+ACT = mybir.ActivationFunctionType
+ALU = mybir.AluOpType
+
+P = 128
+PACK = 4
+K_PASS = P * PACK
+BATCH = 512
+FEATURES = 1024
+K = 2 * FEATURES
+PASSES = K // K_PASS
+ROW_TILES = BATCH // P
+N_TILE = 512
+COL_HALVES = FEATURES // N_TILE
+WORDS_PER_PASS = K_PASS // 2
+
+GATES = ("cand", "input", "forget", "output")
+
+PRODUCT_LAG = 2
+SUM_LAG = 4
+
+FLOPS = 2 * BATCH * K * 4 * FEATURES
+
+
+def tile_quest_pa_kernel(
+    tc,
+    X,
+    hidden1,
+    cell1,
+    Wf1_words,
+    Wf1_scales,
+    bf1,
+    Wi1_words,
+    Wi1_scales,
+    bi1,
+    Wc1_words,
+    Wc1_scales,
+    bc1,
+    Wo1_words,
+    Wo1_scales,
+    bo1,
+    out_0,
+    out_1,
+):
+    nc = tc.nc
+    words_in = {"cand": Wc1_words, "input": Wi1_words, "forget": Wf1_words, "output": Wo1_words}
+    scales_in = {"cand": Wc1_scales, "input": Wi1_scales, "forget": Wf1_scales, "output": Wo1_scales}
+    bias_in = {"cand": bc1, "input": bi1, "forget": bf1, "output": bo1}
+    h_new_out, c_new_out = out_0, out_1
+
+    with ExitStack() as ctx:
+        keep = ctx.enter_context(tc.tile_pool(name="keep", bufs=1))
+        work = ctx.enter_context(tc.tile_pool(name="work", bufs=6))
+        psum = ctx.enter_context(tc.psum_pool(name="psum", bufs=8))
+        ctx.enter_context(tc.manual_schedule())
+
+        warm = keep.tile([P, 1], F32, name="warm")
+        nc.vector.memset(warm[:], 0.0)
+        nc.scalar.activation(out=warm[:], in_=warm[:], func=ACT.Sigmoid)
+        bias_rows = keep.tile([P, len(GATES), FEATURES], BF16, name="bias_rows")
+        nc.vector.memset(bias_rows[:].bitcast(I32), 0)
+        ones = keep.tile([P, P], BF16, name="ones")
+        nc.vector.memset(ones[:], 1.0)
+        w_planes = keep.tile([P, len(GATES), FEATURES], U8, name="w_planes", align_bytes=64)
+        nc.vector.memset(w_planes[:].bitcast(I32), 0)
+        identity = keep.tile([P, P], F32, name="identity")
+        make_identity(nc, identity[:])
+
+        for j, gate in enumerate(GATES):
+            nc.scalar.dma_start(
+                out=bias_rows[0:1, j, :], in_=bias_in[gate].rearrange("(o n) -> o n", o=1)
+            )
+
+        z_rows = []
+        for m in range(ROW_TILES):
+            rows = slice(m * P, (m + 1) * P)
+            z_m = keep.tile([P, K], BF16, name="z_rows_%d" % m)
+            nc.sync.dma_start(out=z_m[:, 0:FEATURES], in_=X[rows, :])
+            nc.sync.dma_start(out=z_m[:, FEATURES:K], in_=hidden1[rows, :])
+            z_rows.append(z_m)
+
+        w_words = {}
+
+        def load_words(gate, half):
+            tile_gh = keep.tile([P, PASSES, N_TILE], U32, name="w_%s_%d" % (gate, half), align_bytes=64)
+            byte_cols = slice(half * N_TILE * PACK, (half + 1) * N_TILE * PACK)
+            src = words_in[gate].rearrange("g p n t -> p g (n t)")[:, :, byte_cols]
+            nc.sync.dma_start(out=tile_gh[:].bitcast(I32), in_=src.bitcast(I32))
+            w_words[gate, half] = tile_gh
+
+        def load_scales(j, gate):
+            for quadrant in range(4):
+                nc.sync.dma_start(
+                    out=w_planes[32 * quadrant : 32 * quadrant + 16, j, :].bitcast(I32),
+                    in_=scales_in[gate][:, 4 * quadrant : 4 * quadrant + 4, :].bitcast(I32),
+                )
+
+        cell_rows = []
+        for j, gate in enumerate(GATES):
+            load_scales(j, gate)
+            load_words(gate, 0)
+            if gate == "forget":
+                for m in range(ROW_TILES):
+                    cell_m = keep.tile([P, FEATURES], BF16, name="cell_%d" % m)
+                    nc.sync.dma_start(out=cell_m[:], in_=cell1[m * P : (m + 1) * P, :])
+                    cell_rows.append(cell_m)
+        for gate in GATES:
+            load_words(gate, 1)
+
+        z_words = []
+        z_planes = []
+        grouped = []
+
+        def quantise(m):
+            codes = keep.tile([P, PASSES * P], U32, name="z_words_%d" % m, align_bytes=64)
+            plane = keep.tile([P, PASSES * P], U8, name="z_plane_%d" % m, align_bytes=64)
+            nc.vector.quantize_mx(out=codes[:].bitcast(FP8X4), scales=plane[:], in_=grouped[m][:])
+            z_words.append(codes)
+            z_planes.append(plane)
+
+        for m in range(ROW_TILES):
+            as_words = z_rows[m][:].bitcast(F32)
+            grouped_m = keep.tile([P, PASSES * P * PACK], BF16, name="grouped_%d" % m, align_bytes=64)
+            grouped.append(grouped_m)
+            for pair in range(PASSES // 2):
+                flipped = psum.tile([P, 2, 2, P], F32, tag="bank", name="flipped")
+                for g_in_pair in range(2):
+                    first = (2 * pair + g_in_pair) * WORDS_PER_PASS
+                    for u in range(2):
+                        nc.tensor.transpose(
+                            flipped[:, g_in_pair, u, :],
+                            as_words[:, first + u : first + WORDS_PER_PASS : 2],
+                            identity[:],
+                        )
+                half_cols = slice(pair * 2 * P * PACK, (pair + 1) * 2 * P * PACK)
+                dst = grouped_m[:, half_cols].bitcast(F32).rearrange("p (g b u) -> p g b u", g=2, u=2)
+                flipped_view = flipped[:].rearrange("p g u b -> p g b u")
+                if pair == 0:
+                    nc.vector.tensor_copy(out=dst, in_=flipped_view)
+                else:
+                    nc.scalar.copy(out=dst, in_=flipped_view)
+            if m >= 1:
+                quantise(m - 1)
+        quantise(ROW_TILES - 1)
+
+        bias_all = []
+        for j in range(len(GATES)):
+            bias_bank = psum.tile([P, FEATURES], BF16, tag="bank", name="bias_bank")
+            for half in range(COL_HALVES):
+                cols = slice(half * N_TILE, (half + 1) * N_TILE)
+                nc.tensor.matmul(out=bias_bank[:, cols], lhsT=ones[:], rhs=bias_rows[:, j, cols], start=True, stop=True)
+            bias_j = keep.tile([P, FEATURES], BF16, name="bias_all_%d" % j)
+            nc.scalar.copy(out=bias_j[:], in_=bias_bank[:])
+            bias_all.append(bias_j)
+
+        steps = [(0, gate, m) for gate in GATES for m in range(ROW_TILES)]
+        steps += [(1, gate, m) for m in range(ROW_TILES) for gate in GATES]
+        gate_tile = {}
+
+        def sums_and_activation(half, gate, m):
+            j = GATES.index(gate)
+            cols = slice(half * N_TILE, (half + 1) * N_TILE)
+            acc = psum.tile([P, N_TILE], F32, tag="bank", name="acc")
+            for g in range(PASSES):
+                batch = slice(g * P, (g + 1) * P)
+                nc.tensor.matmul_mx(
+                    out=acc[:],
+                    lhsT=z_words[m][:, batch].bitcast(FP8X4),
+                    lhsT_scale=z_planes[m][:, batch],
+                    rhs=w_words[gate, half][:, g, :].bitcast(FP8X4),
+                    rhs_scale=w_planes[4 * g : P, j, cols],
+                    start=(g == 0),
+                    stop=(g == PASSES - 1),
+                )
+            t = work.tile([P, N_TILE], F32, tag=gate, name=gate)
+            nc.vector.tensor_tensor(out=t[:], in0=acc[:], in1=bias_all[j][:, cols], op=ALU.add)
+            nc.scalar.activation(out=t[:], in_=t[:], func=(ACT.Tanh if gate == "cand" else ACT.Sigmoid))
+            gate_tile[half, gate, m] = t
+            if gate == "cand":
+                twice = work.tile([P, N_TILE], F32, tag="tanh_cand", name="tanh_cand")
+                nc.scalar.activation(out=twice[:], in_=t[:], func=ACT.Tanh)
+                gate_tile[half, "tanh_cand", m] = twice
+
+        def product(half, gate, m):
+            rows = slice(m * P, (m + 1) * P)
+            cols = slice(half * N_TILE, (half + 1) * N_TILE)
+            t = gate_tile[half, gate, m]
+            if gate == "input":
+                nc.gpsimd.tensor_tensor(out=t[:], in0=t[:], in1=gate_tile[half, "cand", m][:], op=ALU.mult)
+            elif gate == "forget":
+                nc.gpsimd.tensor_tensor(out=t[:], in0=t[:], in1=cell_rows[m][:, cols], op=ALU.mult)
+            elif gate == "output":
+                nc.vector.tensor_tensor(out=t[:], in0=t[:], in1=gate_tile[half, "tanh_cand", m][:], op=ALU.mult)
+                nc.sync.dma_start(out=h_new_out[rows, cols], in_=t[:])
+
+        def cell_sum(half, gate, m):
+            if gate == "forget":
+                rows = slice(m * P, (m + 1) * P)
+                cols = slice(half * N_TILE, (half + 1) * N_TILE)
+                t = gate_tile[half, gate, m]
+                nc.vector.tensor_tensor(out=t[:], in0=t[:], in1=gate_tile[half, "input", m][:], op=ALU.add)
+                nc.sync.dma_start(out=c_new_out[rows, cols], in_=t[:])
+
+        for s in range(len(steps) + SUM_LAG):
+            if s < len(steps):
+                sums_and_activation(*steps[s])
+            if s >= SUM_LAG:
+                cell_sum(*steps[s - SUM_LAG])
+            if PRODUCT_LAG <= s < len(steps) + PRODUCT_LAG:
+                product(*steps[s - PRODUCT_LAG])

@@ -64,6 +64,8 @@ def tile_quest_pa_kernel(
         psum = ctx.enter_context(tc.psum_pool(name="psum", bufs=8))
         ctx.enter_context(tc.manual_schedule())
 
+        w_planes = keep.tile([P, len(GATES), FEATURES], U8, name="w_planes", align_bytes=64)
+        nc.vector.memset(w_planes[:].bitcast(I32), 0)
         warm = keep.tile([P, 1], F32, name="warm")
         nc.vector.memset(warm[:], 0.0)
         nc.scalar.activation(out=warm[:], in_=warm[:], func=ACT.Sigmoid)
@@ -71,15 +73,15 @@ def tile_quest_pa_kernel(
         nc.vector.memset(bias_rows[:].bitcast(I32), 0)
         ones = keep.tile([P, P], BF16, name="ones")
         nc.vector.memset(ones[:], 1.0)
-        w_planes = keep.tile([P, len(GATES), FEATURES], U8, name="w_planes", align_bytes=64)
-        nc.vector.memset(w_planes[:].bitcast(I32), 0)
         identity = keep.tile([P, P], F32, name="identity")
         make_identity(nc, identity[:])
 
         for j, gate in enumerate(GATES):
-            nc.scalar.dma_start(
-                out=bias_rows[0:1, j, :], in_=bias_in[gate].rearrange("(o n) -> o n", o=1)
-            )
+            for quadrant in range(4):
+                nc.gpsimd.dma_start(
+                    out=w_planes[32 * quadrant : 32 * quadrant + 16, j, :].bitcast(F32),
+                    in_=scales_in[gate][:, 4 * quadrant : 4 * quadrant + 4, :].bitcast(F32),
+                )
 
         z_rows = []
         for m in range(ROW_TILES):
@@ -88,6 +90,11 @@ def tile_quest_pa_kernel(
             nc.sync.dma_start(out=z_m[:, 0:FEATURES], in_=X[rows, :])
             nc.sync.dma_start(out=z_m[:, FEATURES:K], in_=hidden1[rows, :])
             z_rows.append(z_m)
+
+        for j, gate in enumerate(GATES):
+            nc.sync.dma_start(
+                out=bias_rows[0:1, j, :], in_=bias_in[gate].rearrange("(o n) -> o n", o=1)
+            )
 
         w_words = {}
 
@@ -98,22 +105,11 @@ def tile_quest_pa_kernel(
             nc.sync.dma_start(out=tile_gh[:].bitcast(I32), in_=src.bitcast(I32))
             w_words[gate, half] = tile_gh
 
-        def load_scales(j, gate):
-            for quadrant in range(4):
-                nc.sync.dma_start(
-                    out=w_planes[32 * quadrant : 32 * quadrant + 16, j, :].bitcast(I32),
-                    in_=scales_in[gate][:, 4 * quadrant : 4 * quadrant + 4, :].bitcast(I32),
-                )
-
-        cell_rows = []
-        for j, gate in enumerate(GATES):
-            load_scales(j, gate)
+        cell_rows = keep.tile([P, ROW_TILES, FEATURES], BF16, name="cell_rows")
+        for gate in GATES:
             load_words(gate, 0)
             if gate == "forget":
-                for m in range(ROW_TILES):
-                    cell_m = keep.tile([P, FEATURES], BF16, name="cell_%d" % m)
-                    nc.sync.dma_start(out=cell_m[:], in_=cell1[m * P : (m + 1) * P, :])
-                    cell_rows.append(cell_m)
+                nc.sync.dma_start(out=cell_rows[:], in_=cell1.rearrange("(m p) n -> p m n", p=P))
         for gate in GATES:
             load_words(gate, 1)
 
@@ -198,7 +194,7 @@ def tile_quest_pa_kernel(
             if gate == "input":
                 nc.gpsimd.tensor_tensor(out=t[:], in0=t[:], in1=gate_tile[half, "cand", m][:], op=ALU.mult)
             elif gate == "forget":
-                nc.gpsimd.tensor_tensor(out=t[:], in0=t[:], in1=cell_rows[m][:, cols], op=ALU.mult)
+                nc.gpsimd.tensor_tensor(out=t[:], in0=t[:], in1=cell_rows[:, m, cols], op=ALU.mult)
             elif gate == "output":
                 nc.vector.tensor_tensor(out=t[:], in0=t[:], in1=gate_tile[half, "tanh_cand", m][:], op=ALU.mult)
                 nc.sync.dma_start(out=h_new_out[rows, cols], in_=t[:])

@@ -26,8 +26,7 @@ WORDS_PER_PASS = K_PASS // 2
 
 GATES = ("cand", "input", "forget", "output")
 
-PRODUCT_LAG = 2
-SUM_LAG = 4
+ROUND_TILES = (2, 1)
 
 FLOPS = 2 * BATCH * K * 4 * FEATURES
 
@@ -76,12 +75,15 @@ def tile_quest_pa_kernel(
         identity = keep.tile([P, P], F32, name="identity")
         make_identity(nc, identity[:])
 
-        for j, gate in enumerate(GATES):
+        def load_scales(j, queue, word):
             for quadrant in range(4):
-                nc.gpsimd.dma_start(
-                    out=w_planes[32 * quadrant : 32 * quadrant + 16, j, :].bitcast(F32),
-                    in_=scales_in[gate][:, 4 * quadrant : 4 * quadrant + 4, :].bitcast(F32),
+                queue.dma_start(
+                    out=w_planes[32 * quadrant : 32 * quadrant + 16, j, :].bitcast(word),
+                    in_=scales_in[GATES[j]][:, 4 * quadrant : 4 * quadrant + 4, :].bitcast(word),
                 )
+
+        for j in range(1, len(GATES)):
+            load_scales(j, nc.gpsimd, F32)
 
         z_rows = []
         for m in range(ROW_TILES):
@@ -96,6 +98,8 @@ def tile_quest_pa_kernel(
                 out=bias_rows[0:1, j, :], in_=bias_in[gate].rearrange("(o n) -> o n", o=1)
             )
 
+        load_scales(0, nc.sync, I32)
+
         w_words = {}
 
         def load_words(gate, half):
@@ -105,11 +109,15 @@ def tile_quest_pa_kernel(
             nc.sync.dma_start(out=tile_gh[:].bitcast(I32), in_=src.bitcast(I32))
             w_words[gate, half] = tile_gh
 
-        cell_rows = keep.tile([P, ROW_TILES, FEATURES], BF16, name="cell_rows")
         for gate in GATES:
             load_words(gate, 0)
-            if gate == "forget":
-                nc.sync.dma_start(out=cell_rows[:], in_=cell1.rearrange("(m p) n -> p m n", p=P))
+        cell_rows = keep.tile([P, ROW_TILES, FEATURES], BF16, name="cell_rows")
+        for first in range(0, ROW_TILES, ROUND_TILES[0]):
+            tiles = slice(first, first + ROUND_TILES[0])
+            batch_rows = slice(first * P, (first + ROUND_TILES[0]) * P)
+            nc.sync.dma_start(
+                out=cell_rows[:, tiles, :], in_=cell1[batch_rows, :].rearrange("(m p) n -> p m n", p=P)
+            )
         for gate in GATES:
             load_words(gate, 1)
 
@@ -159,11 +167,15 @@ def tile_quest_pa_kernel(
             nc.scalar.copy(out=bias_j[:], in_=bias_bank[:])
             bias_all.append(bias_j)
 
-        steps = [(0, gate, m) for gate in GATES for m in range(ROW_TILES)]
-        steps += [(1, gate, m) for m in range(ROW_TILES) for gate in GATES]
+        steps = []
+        for half in range(COL_HALVES):
+            for first in range(0, ROW_TILES, ROUND_TILES[half]):
+                for gate in GATES:
+                    for m in range(first, first + ROUND_TILES[half]):
+                        steps.append((half, gate, m))
         gate_tile = {}
 
-        def sums_and_activation(half, gate, m):
+        def gate_step(half, gate, m):
             j = GATES.index(gate)
             cols = slice(half * N_TILE, (half + 1) * N_TILE)
             acc = psum.tile([P, N_TILE], F32, tag="bank", name="acc")
@@ -179,38 +191,40 @@ def tile_quest_pa_kernel(
                     stop=(g == PASSES - 1),
                 )
             t = work.tile([P, N_TILE], F32, tag=gate, name=gate)
+            gate_tile[half, gate, m] = t
             nc.vector.tensor_tensor(out=t[:], in0=acc[:], in1=bias_all[j][:, cols], op=ALU.add)
             nc.scalar.activation(out=t[:], in_=t[:], func=(ACT.Tanh if gate == "cand" else ACT.Sigmoid))
-            gate_tile[half, gate, m] = t
-            if gate == "cand":
+            if gate == "input":
+                cand = gate_tile[half, "cand", m]
+                nc.gpsimd.tensor_tensor(out=t[:], in0=t[:], in1=cand[:], op=ALU.mult)
                 twice = work.tile([P, N_TILE], F32, tag="tanh_cand", name="tanh_cand")
-                nc.scalar.activation(out=twice[:], in_=t[:], func=ACT.Tanh)
                 gate_tile[half, "tanh_cand", m] = twice
+                nc.scalar.activation(out=twice[:], in_=cand[:], func=ACT.Tanh)
 
-        def product(half, gate, m):
+        def forget_product(half, gate, m):
+            if gate == "forget":
+                cols = slice(half * N_TILE, (half + 1) * N_TILE)
+                t = gate_tile[half, gate, m]
+                nc.vector.tensor_tensor(out=t[:], in0=t[:], in1=cell_rows[:, m, cols], op=ALU.mult)
+
+        def finish(half, gate, m):
             rows = slice(m * P, (m + 1) * P)
             cols = slice(half * N_TILE, (half + 1) * N_TILE)
             t = gate_tile[half, gate, m]
-            if gate == "input":
-                nc.gpsimd.tensor_tensor(out=t[:], in0=t[:], in1=gate_tile[half, "cand", m][:], op=ALU.mult)
-            elif gate == "forget":
-                nc.gpsimd.tensor_tensor(out=t[:], in0=t[:], in1=cell_rows[:, m, cols], op=ALU.mult)
+            if gate == "forget":
+                nc.vector.tensor_tensor(out=t[:], in0=t[:], in1=gate_tile[half, "input", m][:], op=ALU.add)
+                nc.sync.dma_start(out=c_new_out[rows, cols], in_=t[:])
             elif gate == "output":
                 nc.vector.tensor_tensor(out=t[:], in0=t[:], in1=gate_tile[half, "tanh_cand", m][:], op=ALU.mult)
                 nc.sync.dma_start(out=h_new_out[rows, cols], in_=t[:])
 
-        def cell_sum(half, gate, m):
-            if gate == "forget":
-                rows = slice(m * P, (m + 1) * P)
-                cols = slice(half * N_TILE, (half + 1) * N_TILE)
-                t = gate_tile[half, gate, m]
-                nc.vector.tensor_tensor(out=t[:], in0=t[:], in1=gate_tile[half, "input", m][:], op=ALU.add)
-                nc.sync.dma_start(out=c_new_out[rows, cols], in_=t[:])
-
-        for s in range(len(steps) + SUM_LAG):
+        due = [[] for s in range(len(steps) + max(ROUND_TILES) + 2)]
+        for s, step in enumerate(steps):
+            due[s + ROUND_TILES[step[0]] + 1].append(step)
+        for s in range(len(due)):
             if s < len(steps):
-                sums_and_activation(*steps[s])
-            if s >= SUM_LAG:
-                cell_sum(*steps[s - SUM_LAG])
-            if PRODUCT_LAG <= s < len(steps) + PRODUCT_LAG:
-                product(*steps[s - PRODUCT_LAG])
+                gate_step(*steps[s])
+            if 1 <= s <= len(steps):
+                forget_product(*steps[s - 1])
+            for step in due[s]:
+                finish(*step)

@@ -196,12 +196,14 @@ def tile_quest_pa_kernel(
             nc.scalar.activation(out=t[:], in_=t[:], func=(ACT.Tanh if gate == "cand" else ACT.Sigmoid))
             if gate == "input":
                 cand = gate_tile[half, "cand", m]
-                nc.gpsimd.tensor_tensor(out=t[:], in0=t[:], in1=cand[:], op=ALU.mult)
                 twice = work.tile([P, N_TILE], F32, tag="tanh_cand", name="tanh_cand")
                 gate_tile[half, "tanh_cand", m] = twice
                 nc.scalar.activation(out=twice[:], in_=cand[:], func=ACT.Tanh)
 
         def forget_product(half, gate, m):
+            if gate == "input":
+                t = gate_tile[half, gate, m]
+                nc.vector.tensor_tensor(out=t[:], in0=t[:], in1=gate_tile[half, "cand", m][:], op=ALU.mult)
             if gate == "forget":
                 cols = slice(half * N_TILE, (half + 1) * N_TILE)
                 t = gate_tile[half, gate, m]

@@ -26,7 +26,22 @@ WORDS_PER_PASS = K_PASS // 2
 
 GATES = ("cand", "input", "forget", "output")
 
-ROUND_TILES = (2, 1)
+ROUNDS = (
+    (0, 2, 0, 512),
+    (2, 2, 0, 512),
+    (0, 1, 512, 512),
+    (1, 1, 512, 512),
+    (2, 1, 512, 512),
+    (3, 1, 512, 512),
+)
+CI_ON_GPSIMD = (0, 0, 0, 0, 0, 0)
+FC_ON_GPSIMD = (0, 0, 0, 0, 0, 0)
+LAG_CI = 1
+LAG_FC = 1
+LAG_ADD = (3, 3, 2, 2, 2, 2)
+LAG_H = (3, 3, 2, 2, 2, 2)
+
+WARM_UP = 6
 
 FLOPS = 2 * BATCH * K * 4 * FEATURES
 
@@ -63,17 +78,22 @@ def tile_quest_pa_kernel(
         psum = ctx.enter_context(tc.psum_pool(name="psum", bufs=8))
         ctx.enter_context(tc.manual_schedule())
 
+        spin = keep.tile([P, N_TILE], BF16, name="spin")
+        nc.vector.memset(spin[:], 0.0)
+        spin_bank = psum.tile([P, N_TILE], F32, tag="bank", name="spin_bank")
+        for w in range(WARM_UP):
+            nc.tensor.matmul(out=spin_bank[:], lhsT=spin[:, 0:P], rhs=spin[:], start=True, stop=True)
+        bias_rows = keep.tile([P, N_TILE], BF16, name="bias_rows")
+        nc.vector.memset(bias_rows[:], 0.0)
         w_planes = keep.tile([P, len(GATES), FEATURES], U8, name="w_planes", align_bytes=64)
         nc.vector.memset(w_planes[:].bitcast(I32), 0)
         warm = keep.tile([P, 1], F32, name="warm")
         nc.vector.memset(warm[:], 0.0)
         nc.scalar.activation(out=warm[:], in_=warm[:], func=ACT.Sigmoid)
-        bias_rows = keep.tile([P, len(GATES), FEATURES], BF16, name="bias_rows")
-        nc.vector.memset(bias_rows[:].bitcast(I32), 0)
-        ones = keep.tile([P, P], BF16, name="ones")
-        nc.vector.memset(ones[:], 1.0)
         identity = keep.tile([P, P], F32, name="identity")
         make_identity(nc, identity[:])
+        identity_bf = keep.tile([P, P], BF16, name="identity_bf")
+        nc.vector.tensor_copy(out=identity_bf[:], in_=identity[:])
 
         def load_scales(j, queue, word):
             for quadrant in range(4):
@@ -92,11 +112,12 @@ def tile_quest_pa_kernel(
             nc.sync.dma_start(out=z_m[:, 0:FEATURES], in_=X[rows, :])
             nc.sync.dma_start(out=z_m[:, FEATURES:K], in_=hidden1[rows, :])
             z_rows.append(z_m)
-
-        for j, gate in enumerate(GATES):
-            nc.sync.dma_start(
-                out=bias_rows[0:1, j, :], in_=bias_in[gate].rearrange("(o n) -> o n", o=1)
-            )
+            if m == 1:
+                for j, gate in enumerate(GATES):
+                    nc.sync.dma_start(
+                        out=bias_rows[COL_HALVES * j : COL_HALVES * (j + 1), :],
+                        in_=bias_in[gate].rearrange("(h n) -> h n", h=COL_HALVES),
+                    )
 
         load_scales(0, nc.sync, I32)
 
@@ -109,21 +130,45 @@ def tile_quest_pa_kernel(
             nc.sync.dma_start(out=tile_gh[:].bitcast(I32), in_=src.bitcast(I32))
             w_words[gate, half] = tile_gh
 
+        cell_rows = []
+        for half in range(COL_HALVES):
+            cell_half = keep.tile([P, ROW_TILES, N_TILE], BF16, name="cell_rows_%d" % half)
+            cell_rows.append(cell_half)
+
+        def load_cell(first, count, half):
+            cols = slice(half * N_TILE, (half + 1) * N_TILE)
+            nc.sync.dma_start(
+                out=cell_rows[half][:, first : first + count, :],
+                in_=cell1[first * P : (first + count) * P, cols].rearrange("(m p) n -> p m n", p=P),
+            )
+
         for gate in GATES:
             load_words(gate, 0)
-        cell_rows = keep.tile([P, ROW_TILES, FEATURES], BF16, name="cell_rows")
-        for first in range(0, ROW_TILES, ROUND_TILES[0]):
-            tiles = slice(first, first + ROUND_TILES[0])
-            batch_rows = slice(first * P, (first + ROUND_TILES[0]) * P)
-            nc.sync.dma_start(
-                out=cell_rows[:, tiles, :], in_=cell1[batch_rows, :].rearrange("(m p) n -> p m n", p=P)
-            )
+        load_cell(0, 2, 0)
+        load_cell(2, 2, 0)
         for gate in GATES:
             load_words(gate, 1)
+        load_cell(0, 4, 1)
 
         z_words = []
         z_planes = []
         grouped = []
+        bias_all = []
+
+        def spread_bias(j):
+            bias_bank = psum.tile([P, FEATURES], BF16, tag="bank", name="bias_bank")
+            for half in range(COL_HALVES):
+                r = COL_HALVES * j + half
+                nc.tensor.matmul(
+                    out=bias_bank[:, half * N_TILE : (half + 1) * N_TILE],
+                    lhsT=identity_bf[:, r : r + 1].to_broadcast([P, P]),
+                    rhs=bias_rows[:],
+                    start=True,
+                    stop=True,
+                )
+            bias_j = keep.tile([P, FEATURES], BF16, name="bias_all_%d" % j)
+            nc.scalar.copy(out=bias_j[:], in_=bias_bank[:])
+            bias_all.append(bias_j)
 
         def quantise(m):
             codes = keep.tile([P, PASSES * P], U32, name="z_words_%d" % m, align_bytes=64)
@@ -153,80 +198,84 @@ def tile_quest_pa_kernel(
                     nc.vector.tensor_copy(out=dst, in_=flipped_view)
                 else:
                     nc.scalar.copy(out=dst, in_=flipped_view)
+            spread_bias(m)
             if m >= 1:
                 quantise(m - 1)
         quantise(ROW_TILES - 1)
 
-        bias_all = []
-        for j in range(len(GATES)):
-            bias_bank = psum.tile([P, FEATURES], BF16, tag="bank", name="bias_bank")
-            for half in range(COL_HALVES):
-                cols = slice(half * N_TILE, (half + 1) * N_TILE)
-                nc.tensor.matmul(out=bias_bank[:, cols], lhsT=ones[:], rhs=bias_rows[:, j, cols], start=True, stop=True)
-            bias_j = keep.tile([P, FEATURES], BF16, name="bias_all_%d" % j)
-            nc.scalar.copy(out=bias_j[:], in_=bias_bank[:])
-            bias_all.append(bias_j)
-
         steps = []
-        for half in range(COL_HALVES):
-            for first in range(0, ROW_TILES, ROUND_TILES[half]):
-                for gate in GATES:
-                    for m in range(first, first + ROUND_TILES[half]):
-                        steps.append((half, gate, m))
+        late = {}
+
+        def later(s, op, tile_key):
+            late.setdefault(s, []).append((op, tile_key))
+
+        for r, (first, count, start, width) in enumerate(ROUNDS):
+            for gate in GATES:
+                for m in range(first, first + count):
+                    s = len(steps)
+                    key = (m, start, width)
+                    steps.append((gate, key))
+                    if gate == "input":
+                        later(s + LAG_CI, "ci_g" if CI_ON_GPSIMD[r] else "ci_v", key)
+                    if gate == "forget":
+                        later(s + LAG_FC, "fc_g" if FC_ON_GPSIMD[r] else "fc_v", key)
+                        later(s + LAG_ADD[r], "add", key)
+                    if gate == "output":
+                        later(s + LAG_H[r], "h", key)
         gate_tile = {}
 
-        def gate_step(half, gate, m):
+        def gate_step(gate, key):
+            m, start, width = key
             j = GATES.index(gate)
-            cols = slice(half * N_TILE, (half + 1) * N_TILE)
-            acc = psum.tile([P, N_TILE], F32, tag="bank", name="acc")
+            half = start // N_TILE
+            cols = slice(start, start + width)
+            in_half = slice(start - half * N_TILE, start - half * N_TILE + width)
+            acc = psum.tile([P, width], F32, tag="bank", name="acc")
             for g in range(PASSES):
                 batch = slice(g * P, (g + 1) * P)
                 nc.tensor.matmul_mx(
                     out=acc[:],
                     lhsT=z_words[m][:, batch].bitcast(FP8X4),
                     lhsT_scale=z_planes[m][:, batch],
-                    rhs=w_words[gate, half][:, g, :].bitcast(FP8X4),
+                    rhs=w_words[gate, half][:, g, in_half].bitcast(FP8X4),
                     rhs_scale=w_planes[4 * g : P, j, cols],
                     start=(g == 0),
                     stop=(g == PASSES - 1),
                 )
-            t = work.tile([P, N_TILE], F32, tag=gate, name=gate)
-            gate_tile[half, gate, m] = t
+            t = work.tile([P, width], F32, tag=gate, name=gate)
+            gate_tile[gate, key] = t
             nc.vector.tensor_tensor(out=t[:], in0=acc[:], in1=bias_all[j][:, cols], op=ALU.add)
             nc.scalar.activation(out=t[:], in_=t[:], func=(ACT.Tanh if gate == "cand" else ACT.Sigmoid))
             if gate == "input":
-                cand = gate_tile[half, "cand", m]
-                twice = work.tile([P, N_TILE], F32, tag="tanh_cand", name="tanh_cand")
-                gate_tile[half, "tanh_cand", m] = twice
-                nc.scalar.activation(out=twice[:], in_=cand[:], func=ACT.Tanh)
+                twice = work.tile([P, width], F32, tag="tanh_cand", name="tanh_cand")
+                gate_tile["tanh_cand", key] = twice
+                nc.scalar.activation(out=twice[:], in_=gate_tile["cand", key][:], func=ACT.Tanh)
 
-        def forget_product(half, gate, m):
-            if gate == "input":
-                t = gate_tile[half, gate, m]
-                nc.vector.tensor_tensor(out=t[:], in0=t[:], in1=gate_tile[half, "cand", m][:], op=ALU.mult)
-            if gate == "forget":
-                cols = slice(half * N_TILE, (half + 1) * N_TILE)
-                t = gate_tile[half, gate, m]
-                nc.vector.tensor_tensor(out=t[:], in0=t[:], in1=cell_rows[:, m, cols], op=ALU.mult)
-
-        def finish(half, gate, m):
+        def late_op(op, key):
+            m, start, width = key
             rows = slice(m * P, (m + 1) * P)
-            cols = slice(half * N_TILE, (half + 1) * N_TILE)
-            t = gate_tile[half, gate, m]
-            if gate == "forget":
-                nc.vector.tensor_tensor(out=t[:], in0=t[:], in1=gate_tile[half, "input", m][:], op=ALU.add)
+            cols = slice(start, start + width)
+            if op in ("ci_g", "ci_v"):
+                eng = nc.gpsimd if op == "ci_g" else nc.vector
+                t = gate_tile["input", key]
+                eng.tensor_tensor(out=t[:], in0=t[:], in1=gate_tile["cand", key][:], op=ALU.mult)
+            elif op in ("fc_g", "fc_v"):
+                eng = nc.gpsimd if op == "fc_g" else nc.vector
+                t = gate_tile["forget", key]
+                half = start // N_TILE
+                in_half = slice(start - half * N_TILE, start - half * N_TILE + width)
+                eng.tensor_tensor(out=t[:], in0=t[:], in1=cell_rows[half][:, m, in_half], op=ALU.mult)
+            elif op == "add":
+                t = gate_tile["forget", key]
+                nc.vector.tensor_tensor(out=t[:], in0=t[:], in1=gate_tile["input", key][:], op=ALU.add)
                 nc.sync.dma_start(out=c_new_out[rows, cols], in_=t[:])
-            elif gate == "output":
-                nc.vector.tensor_tensor(out=t[:], in0=t[:], in1=gate_tile[half, "tanh_cand", m][:], op=ALU.mult)
+            else:
+                t = gate_tile["output", key]
+                nc.vector.tensor_tensor(out=t[:], in0=t[:], in1=gate_tile["tanh_cand", key][:], op=ALU.mult)
                 nc.sync.dma_start(out=h_new_out[rows, cols], in_=t[:])
 
-        due = [[] for s in range(len(steps) + max(ROUND_TILES) + 2)]
-        for s, step in enumerate(steps):
-            due[s + ROUND_TILES[step[0]] + 1].append(step)
-        for s in range(len(due)):
+        for s in range(max(late) + 1):
             if s < len(steps):
                 gate_step(*steps[s])
-            if 1 <= s <= len(steps):
-                forget_product(*steps[s - 1])
-            for step in due[s]:
-                finish(*step)
+            for op, key in late.get(s, []):
+                late_op(op, key)

@@ -102,8 +102,7 @@ def tile_quest_pa_kernel(
                     in_=scales_in[GATES[j]][:, 4 * quadrant : 4 * quadrant + 4, :].bitcast(word),
                 )
 
-        for j in range(1, len(GATES)):
-            load_scales(j, nc.gpsimd, F32)
+        load_scales(len(GATES) - 1, nc.gpsimd, F32)
 
         z_rows = []
         for m in range(ROW_TILES):
@@ -142,8 +141,10 @@ def tile_quest_pa_kernel(
                 in_=cell1[first * P : (first + count) * P, cols].rearrange("(m p) n -> p m n", p=P),
             )
 
-        for gate in GATES:
+        for j, gate in enumerate(GATES):
             load_words(gate, 0)
+            if j + 1 < len(GATES) - 1:
+                load_scales(j + 1, nc.sync, I32)
         load_cell(0, 2, 0)
         load_cell(2, 2, 0)
         for gate in GATES:

@@ -41,7 +41,6 @@ LAG_FC = 1
 LAG_ADD = (3, 3, 2, 2, 2, 2)
 LAG_H = (3, 3, 2, 2, 2, 2)
 
-WARM_UP = 6
 
 FLOPS = 2 * BATCH * K * 4 * FEATURES
 
@@ -78,11 +77,6 @@ def tile_quest_pa_kernel(
         psum = ctx.enter_context(tc.psum_pool(name="psum", bufs=8))
         ctx.enter_context(tc.manual_schedule())
 
-        spin = keep.tile([P, N_TILE], BF16, name="spin")
-        nc.vector.memset(spin[:], 0.0)
-        spin_bank = psum.tile([P, N_TILE], F32, tag="bank", name="spin_bank")
-        for w in range(WARM_UP):
-            nc.tensor.matmul(out=spin_bank[:], lhsT=spin[:, 0:P], rhs=spin[:], start=True, stop=True)
         bias_rows = keep.tile([P, N_TILE], BF16, name="bias_rows")
         nc.vector.memset(bias_rows[:], 0.0)
         w_planes = keep.tile([P, len(GATES), FEATURES], U8, name="w_planes", align_bytes=64)
@@ -199,9 +193,10 @@ def tile_quest_pa_kernel(
                     nc.vector.tensor_copy(out=dst, in_=flipped_view)
                 else:
                     nc.scalar.copy(out=dst, in_=flipped_view)
-            spread_bias(m)
             if m >= 1:
                 quantise(m - 1)
+        for j in range(len(GATES)):
+            spread_bias(j)
         quantise(ROW_TILES - 1)
 
         steps = []

@@ -96,6 +96,7 @@ def tile_quest_pa_kernel(
                     in_=scales_in[GATES[j]][:, 4 * quadrant : 4 * quadrant + 4, :].bitcast(word),
                 )
 
+        load_scales(0, nc.gpsimd, F32)
         load_scales(len(GATES) - 1, nc.gpsimd, F32)
 
         z_rows = []
@@ -111,8 +112,6 @@ def tile_quest_pa_kernel(
                         out=bias_rows[COL_HALVES * j : COL_HALVES * (j + 1), :],
                         in_=bias_in[gate].rearrange("(h n) -> h n", h=COL_HALVES),
                     )
-
-        load_scales(0, nc.sync, I32)
 
         w_words = {}
 

@@ -27,8 +27,8 @@ WORDS_PER_PASS = K_PASS // 2
 GATES = ("cand", "input", "forget", "output")
 
 ROUNDS = (
-    (0, 2, 0, 512),
-    (2, 2, 0, 512),
+    (0, 3, 0, 512),
+    (3, 1, 0, 512),
     (0, 1, 512, 512),
     (1, 1, 512, 512),
     (2, 1, 512, 512),
@@ -38,8 +38,8 @@ CI_ON_GPSIMD = (0, 0, 0, 0, 0, 0)
 FC_ON_GPSIMD = (0, 0, 0, 0, 0, 0)
 LAG_CI = 1
 LAG_FC = 1
-LAG_ADD = (3, 3, 2, 2, 2, 2)
-LAG_H = (3, 3, 2, 2, 2, 2)
+LAG_ADD = (4, 2, 2, 2, 2, 2)
+LAG_H = (4, 2, 2, 2, 2, 2)
 
 
 FLOPS = 2 * BATCH * K * 4 * FEATURES

@@ -40,6 +40,8 @@ LAG_CI = 1
 LAG_FC = 1
 LAG_ADD = (4, 2, 2, 2, 2, 2)
 LAG_H = (4, 2, 2, 2, 2, 2)
+FIRST_PIECES = 4
+BIAS_BEHIND = ((), (0,), (1, 2), (3,))
 
 
 FLOPS = 2 * BATCH * K * 4 * FEATURES
@@ -115,12 +117,18 @@ def tile_quest_pa_kernel(
 
         w_words = {}
 
-        def load_words(gate, half):
-            tile_gh = keep.tile([P, PASSES, N_TILE], U32, name="w_%s_%d" % (gate, half), align_bytes=64)
+        def load_words(gate, half, pieces):
             byte_cols = slice(half * N_TILE * PACK, (half + 1) * N_TILE * PACK)
             src = words_in[gate].rearrange("g p n t -> p g (n t)")[:, :, byte_cols]
-            nc.sync.dma_start(out=tile_gh[:].bitcast(I32), in_=src.bitcast(I32))
-            w_words[gate, half] = tile_gh
+            per_piece = PASSES // pieces
+            operands = []
+            for c in range(pieces):
+                tile_c = keep.tile([P, per_piece, N_TILE], U32, name="w_%s_%d_%d" % (gate, half, c), align_bytes=64)
+                part = src[:, c * per_piece : (c + 1) * per_piece, :]
+                nc.sync.dma_start(out=tile_c[:].bitcast(I32), in_=part.bitcast(I32))
+                for g in range(per_piece):
+                    operands.append(tile_c[:, g, :])
+            w_words[gate, half] = operands
 
         cell_rows = []
         for half in range(COL_HALVES):
@@ -135,13 +143,13 @@ def tile_quest_pa_kernel(
             )
 
         for j, gate in enumerate(GATES):
-            load_words(gate, 0)
+            load_words(gate, 0, FIRST_PIECES if j == 0 else 1)
             if j + 1 < len(GATES) - 1:
                 load_scales(j + 1, nc.sync, I32)
         load_cell(0, 2, 0)
         load_cell(2, 2, 0)
         for gate in GATES:
-            load_words(gate, 1)
+            load_words(gate, 1, 1)
         load_cell(0, 4, 1)
 
         z_words = []
@@ -192,10 +200,10 @@ def tile_quest_pa_kernel(
                     nc.vector.tensor_copy(out=dst, in_=flipped_view)
                 else:
                     nc.scalar.copy(out=dst, in_=flipped_view)
+            for j in BIAS_BEHIND[m]:
+                spread_bias(j)
             if m >= 1:
                 quantise(m - 1)
-        for j in range(len(GATES)):
-            spread_bias(j)
         quantise(ROW_TILES - 1)
 
         steps = []
@@ -219,24 +227,37 @@ def tile_quest_pa_kernel(
                         later(s + LAG_H[r], "h", key)
         gate_tile = {}
 
-        def gate_step(gate, key):
+        def one_pass(acc, gate, key, g):
             m, start, width = key
             j = GATES.index(gate)
             half = start // N_TILE
             cols = slice(start, start + width)
             in_half = slice(start - half * N_TILE, start - half * N_TILE + width)
-            acc = psum.tile([P, width], F32, tag="bank", name="acc")
+            batch = slice(g * P, (g + 1) * P)
+            nc.tensor.matmul_mx(
+                out=acc[:],
+                lhsT=z_words[m][:, batch].bitcast(FP8X4),
+                lhsT_scale=z_planes[m][:, batch],
+                rhs=w_words[gate, half][g][:, in_half].bitcast(FP8X4),
+                rhs_scale=w_planes[4 * g : P, j, cols],
+                start=(g == 0),
+                stop=(g == PASSES - 1),
+            )
+
+        def sums(group):
+            banks = []
+            for gate, key in group:
+                acc = psum.tile([P, key[2]], F32, tag="bank", name="acc")
+                banks.append(acc)
             for g in range(PASSES):
-                batch = slice(g * P, (g + 1) * P)
-                nc.tensor.matmul_mx(
-                    out=acc[:],
-                    lhsT=z_words[m][:, batch].bitcast(FP8X4),
-                    lhsT_scale=z_planes[m][:, batch],
-                    rhs=w_words[gate, half][:, g, in_half].bitcast(FP8X4),
-                    rhs_scale=w_planes[4 * g : P, j, cols],
-                    start=(g == 0),
-                    stop=(g == PASSES - 1),
-                )
+                for acc, (gate, key) in zip(banks, group):
+                    one_pass(acc, gate, key, g)
+            return banks
+
+        def gate_step(acc, gate, key):
+            m, start, width = key
+            j = GATES.index(gate)
+            cols = slice(start, start + width)
             t = work.tile([P, width], F32, tag=gate, name=gate)
             gate_tile[gate, key] = t
             nc.vector.tensor_tensor(out=t[:], in0=acc[:], in1=bias_all[j][:, cols], op=ALU.add)
@@ -269,8 +290,13 @@ def tile_quest_pa_kernel(
                 nc.vector.tensor_tensor(out=t[:], in0=t[:], in1=gate_tile["tanh_cand", key][:], op=ALU.mult)
                 nc.sync.dma_start(out=h_new_out[rows, cols], in_=t[:])
 
+        banks_of = {}
         for s in range(max(late) + 1):
             if s < len(steps):
-                gate_step(*steps[s])
+                if s not in banks_of:
+                    group = steps[s : s + (ROUNDS[0][1] if s == 0 else 1)]
+                    for k, acc in enumerate(sums(group)):
+                        banks_of[s + k] = acc
+                gate_step(banks_of[s], *steps[s])
             for op, key in late.get(s, []):
                 late_op(op, key)

@@ -41,7 +41,8 @@ LAG_FC = 1
 LAG_ADD = (4, 2, 2, 2, 2, 2)
 LAG_H = (4, 2, 2, 2, 2, 2)
 FIRST_PIECES = 4
-BIAS_BEHIND = ((), (0,), (1, 2), (3,))
+BIAS_BEHIND_TILE = {1: ((0, 0),), 2: ((1, 0), (2, 0)), 3: ((3, 0),)}
+BIAS_BEHIND_STEP = {}
 
 
 FLOPS = 2 * BATCH * K * 4 * FEATURES
@@ -148,29 +149,30 @@ def tile_quest_pa_kernel(
                 load_scales(j + 1, nc.sync, I32)
         load_cell(0, 2, 0)
         load_cell(2, 2, 0)
-        for gate in GATES:
+        bias_all = {}
+        for j, gate in enumerate(GATES):
             load_words(gate, 1, 1)
+            bias_j1 = keep.tile([P, N_TILE], BF16, name="bias_all_%d_1" % j)
+            nc.sync.dma_start(out=bias_j1[:], in_=bias_in[gate][N_TILE:FEATURES].partition_broadcast(P))
+            bias_all[j, 1] = bias_j1
         load_cell(0, 4, 1)
 
         z_words = []
         z_planes = []
         grouped = []
-        bias_all = []
-
-        def spread_bias(j):
-            bias_bank = psum.tile([P, FEATURES], BF16, tag="bank", name="bias_bank")
-            for half in range(COL_HALVES):
-                r = COL_HALVES * j + half
-                nc.tensor.matmul(
-                    out=bias_bank[:, half * N_TILE : (half + 1) * N_TILE],
-                    lhsT=identity_bf[:, r : r + 1].to_broadcast([P, P]),
-                    rhs=bias_rows[:],
-                    start=True,
-                    stop=True,
-                )
-            bias_j = keep.tile([P, FEATURES], BF16, name="bias_all_%d" % j)
-            nc.scalar.copy(out=bias_j[:], in_=bias_bank[:])
-            bias_all.append(bias_j)
+        def spread_bias(j, half):
+            bias_bank = psum.tile([P, N_TILE], BF16, tag="bank", name="bias_bank")
+            r = COL_HALVES * j + half
+            nc.tensor.matmul(
+                out=bias_bank[:],
+                lhsT=identity_bf[:, r : r + 1].to_broadcast([P, P]),
+                rhs=bias_rows[:],
+                start=True,
+                stop=True,
+            )
+            bias_jh = keep.tile([P, N_TILE], BF16, name="bias_all_%d_%d" % (j, half))
+            nc.scalar.copy(out=bias_jh[:], in_=bias_bank[:])
+            bias_all[j, half] = bias_jh
 
         def quantise(m):
             codes = keep.tile([P, PASSES * P], U32, name="z_words_%d" % m, align_bytes=64)
@@ -200,8 +202,8 @@ def tile_quest_pa_kernel(
                     nc.vector.tensor_copy(out=dst, in_=flipped_view)
                 else:
                     nc.scalar.copy(out=dst, in_=flipped_view)
-            for j in BIAS_BEHIND[m]:
-                spread_bias(j)
+            for j, half in BIAS_BEHIND_TILE.get(m, ()):
+                spread_bias(j, half)
             if m >= 1:
                 quantise(m - 1)
         quantise(ROW_TILES - 1)
@@ -260,7 +262,9 @@ def tile_quest_pa_kernel(
             cols = slice(start, start + width)
             t = work.tile([P, width], F32, tag=gate, name=gate)
             gate_tile[gate, key] = t
-            nc.vector.tensor_tensor(out=t[:], in0=acc[:], in1=bias_all[j][:, cols], op=ALU.add)
+            half = start // N_TILE
+            in_half = slice(start - half * N_TILE, start - half * N_TILE + width)
+            nc.vector.tensor_tensor(out=t[:], in0=acc[:], in1=bias_all[j, half][:, in_half], op=ALU.add)
             nc.scalar.activation(out=t[:], in_=t[:], func=(ACT.Tanh if gate == "cand" else ACT.Sigmoid))
             if gate == "input":
                 twice = work.tile([P, width], F32, tag="tanh_cand", name="tanh_cand")
@@ -297,6 +301,8 @@ def tile_quest_pa_kernel(
                     group = steps[s : s + (ROUNDS[0][1] if s == 0 else 1)]
                     for k, acc in enumerate(sums(group)):
                         banks_of[s + k] = acc
+                for j, half in BIAS_BEHIND_STEP.get(s, ()):
+                    spread_bias(j, half)
                 gate_step(banks_of[s], *steps[s])
             for op, key in late.get(s, []):
                 late_op(op, key)

from contextlib import ExitStack

import concourse.mybir as mybir
from concourse.masks import make_identity

F32 = mybir.dt.float32
BF16 = mybir.dt.bfloat16
I32 = mybir.dt.int32
U32 = mybir.dt.uint32
U8 = mybir.dt.uint8
FP8X4 = mybir.dt.float8_e4m3fn_x4
ACT = mybir.ActivationFunctionType
ALU = mybir.AluOpType

P = 128
PACK = 4
K_PASS = P * PACK
BATCH = 512
FEATURES = 1024
K = 2 * FEATURES
PASSES = K // K_PASS
ROW_TILES = BATCH // P
N_TILE = 512
COL_HALVES = FEATURES // N_TILE
WORDS_PER_PASS = K_PASS // 2

GATES = ("cand", "input", "forget", "output")

ROUNDS = (
    (0, 3, 0, 512),
    (3, 1, 0, 512),
    (0, 1, 512, 512),
    (1, 1, 512, 512),
    (2, 1, 512, 512),
    (3, 1, 512, 512),
)
CI_ON_GPSIMD = (0, 0, 0, 0, 0, 0)
FC_ON_GPSIMD = (0, 0, 0, 0, 0, 0)
LAG_CI = 1
LAG_FC = 1
LAG_ADD = (4, 2, 2, 2, 2, 2)
LAG_H = (4, 2, 2, 2, 2, 2)
FIRST_PIECES = 4
BIAS_BEHIND_TILE = {1: ((0, 0),), 2: ((1, 0), (2, 0)), 3: ((3, 0),)}
BIAS_BEHIND_STEP = {}


FLOPS = 2 * BATCH * K * 4 * FEATURES


def tile_quest_pa_kernel(
    tc,
    X,
    hidden1,
    cell1,
    Wf1_words,
    Wf1_scales,
    bf1,
    Wi1_words,
    Wi1_scales,
    bi1,
    Wc1_words,
    Wc1_scales,
    bc1,
    Wo1_words,
    Wo1_scales,
    bo1,
    out_0,
    out_1,
):
    nc = tc.nc
    words_in = {"cand": Wc1_words, "input": Wi1_words, "forget": Wf1_words, "output": Wo1_words}
    scales_in = {"cand": Wc1_scales, "input": Wi1_scales, "forget": Wf1_scales, "output": Wo1_scales}
    bias_in = {"cand": bc1, "input": bi1, "forget": bf1, "output": bo1}
    h_new_out, c_new_out = out_0, out_1

    with ExitStack() as ctx:
        keep = ctx.enter_context(tc.tile_pool(name="keep", bufs=1))
        work = ctx.enter_context(tc.tile_pool(name="work", bufs=6))
        psum = ctx.enter_context(tc.psum_pool(name="psum", bufs=8))
        ctx.enter_context(tc.manual_schedule())

        bias_rows = keep.tile([P, N_TILE], BF16, name="bias_rows")
        nc.vector.memset(bias_rows[:], 0.0)
        w_planes = keep.tile([P, len(GATES), FEATURES], U8, name="w_planes", align_bytes=64)
        nc.vector.memset(w_planes[:].bitcast(I32), 0)
        warm = keep.tile([P, 1], F32, name="warm")
        nc.vector.memset(warm[:], 0.0)
        nc.scalar.activation(out=warm[:], in_=warm[:], func=ACT.Sigmoid)
        identity = keep.tile([P, P], F32, name="identity")
        make_identity(nc, identity[:])
        identity_bf = keep.tile([P, P], BF16, name="identity_bf")
        nc.vector.tensor_copy(out=identity_bf[:], in_=identity[:])

        def load_scales(j, queue, word):
            for quadrant in range(4):
                queue.dma_start(
                    out=w_planes[32 * quadrant : 32 * quadrant + 16, j, :].bitcast(word),
                    in_=scales_in[GATES[j]][:, 4 * quadrant : 4 * quadrant + 4, :].bitcast(word),
                )

        load_scales(0, nc.gpsimd, F32)
        load_scales(len(GATES) - 1, nc.gpsimd, F32)

        z_rows = []
        for m in range(ROW_TILES):
            rows = slice(m * P, (m + 1) * P)
            z_m = keep.tile([P, K], BF16, name="z_rows_%d" % m)
            nc.sync.dma_start(out=z_m[:, 0:FEATURES], in_=X[rows, :])
            nc.sync.dma_start(out=z_m[:, FEATURES:K], in_=hidden1[rows, :])
            z_rows.append(z_m)
            if m == 1:
                for j, gate in enumerate(GATES):
                    nc.sync.dma_start(
                        out=bias_rows[COL_HALVES * j : COL_HALVES * (j + 1), :],
                        in_=bias_in[gate].rearrange("(h n) -> h n", h=COL_HALVES),
                    )

        w_words = {}

        def load_words(gate, half, pieces):
            byte_cols = slice(half * N_TILE * PACK, (half + 1) * N_TILE * PACK)
            src = words_in[gate].rearrange("g p n t -> p g (n t)")[:, :, byte_cols]
            per_piece = PASSES // pieces
            operands = []
            for c in range(pieces):
                tile_c = keep.tile([P, per_piece, N_TILE], U32, name="w_%s_%d_%d" % (gate, half, c), align_bytes=64)
                part = src[:, c * per_piece : (c + 1) * per_piece, :]
                nc.sync.dma_start(out=tile_c[:].bitcast(I32), in_=part.bitcast(I32))
                for g in range(per_piece):
                    operands.append(tile_c[:, g, :])
            w_words[gate, half] = operands

        cell_rows = []
        for half in range(COL_HALVES):
            cell_half = keep.tile([P, ROW_TILES, N_TILE], BF16, name="cell_rows_%d" % half)
            cell_rows.append(cell_half)

        def load_cell(first, count, half):
            cols = slice(half * N_TILE, (half + 1) * N_TILE)
            nc.sync.dma_start(
                out=cell_rows[half][:, first : first + count, :],
                in_=cell1[first * P : (first + count) * P, cols].rearrange("(m p) n -> p m n", p=P),
            )

        for j, gate in enumerate(GATES):
            load_words(gate, 0, FIRST_PIECES if j == 0 else 1)
            if j + 1 < len(GATES) - 1:
                load_scales(j + 1, nc.sync, I32)
        load_cell(0, 2, 0)
        load_cell(2, 2, 0)
        bias_all = {}
        for j, gate in enumerate(GATES):
            load_words(gate, 1, 1)
            bias_j1 = keep.tile([P, N_TILE], BF16, name="bias_all_%d_1" % j)
            nc.sync.dma_start(out=bias_j1[:], in_=bias_in[gate][N_TILE:FEATURES].partition_broadcast(P))
            bias_all[j, 1] = bias_j1
        load_cell(0, 4, 1)

        z_words = []
        z_planes = []
        grouped = []
        def spread_bias(j, half):
            bias_bank = psum.tile([P, N_TILE], BF16, tag="bank", name="bias_bank")
            r = COL_HALVES * j + half
            nc.tensor.matmul(
                out=bias_bank[:],
                lhsT=identity_bf[:, r : r + 1].to_broadcast([P, P]),
                rhs=bias_rows[:],
                start=True,
                stop=True,
            )
            bias_jh = keep.tile([P, N_TILE], BF16, name="bias_all_%d_%d" % (j, half))
            nc.scalar.copy(out=bias_jh[:], in_=bias_bank[:])
            bias_all[j, half] = bias_jh

        def quantise(m):
            codes = keep.tile([P, PASSES * P], U32, name="z_words_%d" % m, align_bytes=64)
            plane = keep.tile([P, PASSES * P], U8, name="z_plane_%d" % m, align_bytes=64)
            nc.vector.quantize_mx(out=codes[:].bitcast(FP8X4), scales=plane[:], in_=grouped[m][:])
            z_words.append(codes)
            z_planes.append(plane)

        for m in range(ROW_TILES):
            as_words = z_rows[m][:].bitcast(F32)
            grouped_m = keep.tile([P, PASSES * P * PACK], BF16, name="grouped_%d" % m, align_bytes=64)
            grouped.append(grouped_m)
            for pair in range(PASSES // 2):
                flipped = psum.tile([P, 2, 2, P], F32, tag="bank", name="flipped")
                for g_in_pair in range(2):
                    first = (2 * pair + g_in_pair) * WORDS_PER_PASS
                    for u in range(2):
                        nc.tensor.transpose(
                            flipped[:, g_in_pair, u, :],
                            as_words[:, first + u : first + WORDS_PER_PASS : 2],
                            identity[:],
                        )
                half_cols = slice(pair * 2 * P * PACK, (pair + 1) * 2 * P * PACK)
                dst = grouped_m[:, half_cols].bitcast(F32).rearrange("p (g b u) -> p g b u", g=2, u=2)
                flipped_view = flipped[:].rearrange("p g u b -> p g b u")
                if pair == 0:
                    nc.vector.tensor_copy(out=dst, in_=flipped_view)
                else:
                    nc.scalar.copy(out=dst, in_=flipped_view)
            for j, half in BIAS_BEHIND_TILE.get(m, ()):
                spread_bias(j, half)
            if m >= 1:
                quantise(m - 1)
        quantise(ROW_TILES - 1)

        steps = []
        late = {}

        def later(s, op, tile_key):
            late.setdefault(s, []).append((op, tile_key))

        for r, (first, count, start, width) in enumerate(ROUNDS):
            for gate in GATES:
                for m in range(first, first + count):
                    s = len(steps)
                    key = (m, start, width)
                    steps.append((gate, key))
                    if gate == "input":
                        later(s + LAG_CI, "ci_g" if CI_ON_GPSIMD[r] else "ci_v", key)
                    if gate == "forget":
                        later(s + LAG_FC, "fc_g" if FC_ON_GPSIMD[r] else "fc_v", key)
                        later(s + LAG_ADD[r], "add", key)
                    if gate == "output":
                        later(s + LAG_H[r], "h", key)
        gate_tile = {}

        def one_pass(acc, gate, key, g):
            m, start, width = key
            j = GATES.index(gate)
            half = start // N_TILE
            cols = slice(start, start + width)
            in_half = slice(start - half * N_TILE, start - half * N_TILE + width)
            batch = slice(g * P, (g + 1) * P)
            nc.tensor.matmul_mx(
                out=acc[:],
                lhsT=z_words[m][:, batch].bitcast(FP8X4),
                lhsT_scale=z_planes[m][:, batch],
                rhs=w_words[gate, half][g][:, in_half].bitcast(FP8X4),
                rhs_scale=w_planes[4 * g : P, j, cols],
                start=(g == 0),
                stop=(g == PASSES - 1),
            )

        def sums(group):
            banks = []
            for gate, key in group:
                acc = psum.tile([P, key[2]], F32, tag="bank", name="acc")
                banks.append(acc)
            for g in range(PASSES):
                for acc, (gate, key) in zip(banks, group):
                    one_pass(acc, gate, key, g)
            return banks

        def gate_step(acc, gate, key):
            m, start, width = key
            j = GATES.index(gate)
            cols = slice(start, start + width)
            t = work.tile([P, width], F32, tag=gate, name=gate)
            gate_tile[gate, key] = t
            half = start // N_TILE
            in_half = slice(start - half * N_TILE, start - half * N_TILE + width)
            nc.vector.tensor_tensor(out=t[:], in0=acc[:], in1=bias_all[j, half][:, in_half], op=ALU.add)
            nc.scalar.activation(out=t[:], in_=t[:], func=(ACT.Tanh if gate == "cand" else ACT.Sigmoid))
            if gate == "input":
                twice = work.tile([P, width], F32, tag="tanh_cand", name="tanh_cand")
                gate_tile["tanh_cand", key] = twice
                nc.scalar.activation(out=twice[:], in_=gate_tile["cand", key][:], func=ACT.Tanh)

        def late_op(op, key):
            m, start, width = key
            rows = slice(m * P, (m + 1) * P)
            cols = slice(start, start + width)
            if op in ("ci_g", "ci_v"):
                eng = nc.gpsimd if op == "ci_g" else nc.vector
                t = gate_tile["input", key]
                eng.tensor_tensor(out=t[:], in0=t[:], in1=gate_tile["cand", key][:], op=ALU.mult)
            elif op in ("fc_g", "fc_v"):
                eng = nc.gpsimd if op == "fc_g" else nc.vector
                t = gate_tile["forget", key]
                half = start // N_TILE
                in_half = slice(start - half * N_TILE, start - half * N_TILE + width)
                eng.tensor_tensor(out=t[:], in0=t[:], in1=cell_rows[half][:, m, in_half], op=ALU.mult)
            elif op == "add":
                t = gate_tile["forget", key]
                nc.vector.tensor_tensor(out=t[:], in0=t[:], in1=gate_tile["input", key][:], op=ALU.add)
                nc.sync.dma_start(out=c_new_out[rows, cols], in_=t[:])
            else:
                t = gate_tile["output", key]
                nc.vector.tensor_tensor(out=t[:], in0=t[:], in1=gate_tile["tanh_cand", key][:], op=ALU.mult)
                nc.sync.dma_start(out=h_new_out[rows, cols], in_=t[:])

        banks_of = {}
        for s in range(max(late) + 1):
            if s < len(steps):
                if s not in banks_of:
                    group = steps[s : s + (ROUNDS[0][1] if s == 0 else 1)]
                    for k, acc in enumerate(sums(group)):
                        banks_of[s + k] = acc
                for j, half in BIAS_BEHIND_STEP.get(s, ()):
                    spread_bias(j, half)
                gate_step(banks_of[s], *steps[s])
            for op, key in late.get(s, []):
                late_op(op, key)
